import numpy as np
import ml_dtypes


def mxq(x, axis, fmt="e4m3"):
    dtype, down = {"e4m3": (ml_dtypes.float8_e4m3fn, 7), "e5m2": (ml_dtypes.float8_e5m2, 14)}[fmt]
    v = np.moveaxis(np.asarray(x, np.float32).astype(ml_dtypes.bfloat16).astype(np.float64), axis, -1)
    blocks = v.reshape(v.shape[:-1] + (-1, 32))
    amax = np.abs(blocks).max(-1, keepdims=True)
    byte = np.maximum(np.where(amax > 0, np.frexp(amax)[1] - 1 + 127, 0) - down, 1)
    scale = np.exp2(byte - 127.0)
    codes = (blocks / scale).astype(np.float32).astype(dtype).astype(np.float64)
    return np.moveaxis((codes * scale).reshape(v.shape), -1, axis)


WIDE = False


def mx_kscale(k):
    if not WIDE:
        return np.ones(k)
    levels = np.array([10, -10, 5, -5, 0])
    a = np.random.permutation(np.resize(levels, k // 512 * 4)).reshape(k // 512, 4)
    idx = np.arange(k)
    return np.exp2(a[idx // 512, idx % 128 // 32])


BF16 = ml_dtypes.bfloat16


def bf(x):
    return np.asarray(x, np.float32).astype(BF16)


def f64(x):
    return np.asarray(x).astype(np.float64)


E2M1 = np.array([0.0, 0.5, 1.0, 1.5, 2.0, 3.0, 4.0, 6.0, -0.0, -0.5, -1.0, -1.5, -2.0, -3.0, -4.0, -6.0])


def pack_weight(w, fmt):
    k, n = w.shape
    w = f64(bf(w)).reshape(k // 32, 32, n)
    amax = np.abs(w).max(1)
    if fmt == "e4m3":
        byte = np.frexp(amax)[1] - 1 + 127 - 7
    else:
        mant, ex = np.frexp(amax / 6.0)
        byte = np.where(mant > 0.5, ex, ex - 1) + 127
    byte = np.clip(np.where(amax > 0, byte, 1), 1, 254)
    scaled = (w * np.exp2(127.0 - byte)[:, None, :]).reshape(k, n).astype(np.float32)
    by_word = np.ascontiguousarray(scaled.reshape(k // 512, 128, 4, n).transpose(0, 1, 3, 2))
    if fmt == "e4m3":
        words = by_word.astype(ml_dtypes.float8_e4m3fn).view(np.uint8)
    else:
        c = by_word.astype(ml_dtypes.float4_e2m1fn).view(np.uint8) & 0xF
        words = c[..., 0::2] | (c[..., 1::2] << 4)
    return np.ascontiguousarray(words), np.ascontiguousarray(byte.astype(np.uint8).reshape(k // 512, 16, n))


def unpack_weight(words, scales, fmt):
    g, p, n, _ = words.shape
    if fmt == "e4m3":
        vals = np.ascontiguousarray(words).view(ml_dtypes.float8_e4m3fn).astype(np.float64)
    else:
        nib = np.empty((g, p, n, 4), np.uint8)
        nib[..., 0::2] = words & 0xF
        nib[..., 1::2] = words >> 4
        vals = E2M1[nib]
    vals = vals * np.repeat(np.exp2(scales.astype(np.float64) - 127.0), 8, axis=1)[..., None]
    return vals.transpose(0, 1, 3, 2).reshape(g * 512, n)

def pack4(w):
    words, scales = pack_weight(w, "e2m1")
    return words.reshape(words.shape[0], 128, -1), scales


def unpack4(words, scales):
    return unpack_weight(words.reshape(words.shape[0], 128, -1, 2), scales, "e2m1")


B, S, IN, OUT, A, R = 8, 1024, 1024, 128, 8, 128
G = B // A
SCALING = 2.0


def setup_inputs():
    s = mx_kscale(IN)
    data = bf(np.random.standard_normal((B, S, IN)) * s)
    w = np.random.standard_normal((OUT, IN)) / np.sqrt(IN) / s
    W_words, W_scales = pack4(np.ascontiguousarray(w.T))
    t_lora = bf(np.random.standard_normal((A, G, S, R)))
    lora_b = bf(np.random.standard_normal((A, OUT, R)) * 0.5 / np.sqrt(R))
    return {"data": data,
            "W_words": W_words,
            "W_scales": W_scales,
            "t_lora": t_lora,
            "lora_b": lora_b}


def reference(data, W_words, W_scales, t_lora, lora_b):
    base = mxq(f64(data), 2, "e4m3") @ unpack4(W_words, W_scales)
    delta = (f64(t_lora).reshape(A, G * S, R) @ f64(lora_b).transpose(0, 2, 1)) * SCALING
    return base + delta.reshape(B, S, OUT)

@@ -1,0 +1,166 @@
+from contextlib import ExitStack
+
+import concourse.mybir as mybir
+from concourse.masks import make_identity
+
+BF16 = mybir.dt.bfloat16
+F32 = mybir.dt.float32
+I32 = mybir.dt.int32
+U8 = mybir.dt.uint8
+U32 = mybir.dt.uint32
+FP8X4 = mybir.dt.float8_e4m3fn_x4
+FP4X4 = mybir.dt.float4_e2m1fn_x4
+MULT = mybir.AluOpType.mult
+ADD = mybir.AluOpType.add
+
+P = 128
+PACK = 4
+HALVES = 2
+ADAPTERS, SEQ, IN, OUT, RANK = 8, 1024, 1024, 128, 128
+SCALING = 2.0
+TOKENS = ADAPTERS * SEQ
+PASSES = IN // (P * PACK)
+WORDS_PER_PASS = P * HALVES
+TILES = 4
+CHUNK = TILES * P
+CHUNKS = TOKENS // CHUNK
+CHUNKS_PER_ADAPTER = SEQ // CHUNK
+SCALAR_COPIES = 3
+QUADRANTS = 4
+
+FLOPS = 2 * TOKENS * IN * OUT + 2 * TOKENS * RANK * OUT
+
+
+def chunk_view(rows, c):
+    return rows[c * CHUNK : (c + 1) * CHUNK, :].rearrange("(p j) w -> p j w", j=TILES)
+
+
+def tile_linear_pa_t_kernel(tc, data, W_words, W_scales, t_lora, lora_b, out):
+    nc = tc.nc
+    x_rows = data.rearrange("b s i -> (b s) i")
+    t_rows = t_lora.rearrange("a g s r -> (a g s) r")
+    out_rows = out.rearrange("b s o -> (b s) o")
+
+    with ExitStack() as ctx:
+        ctx.enter_context(tc.manual_schedule())
+        const = ctx.enter_context(tc.tile_pool(name="const", bufs=1))
+        resident = ctx.enter_context(tc.tile_pool(name="resident", bufs=CHUNKS))
+        stage = ctx.enter_context(tc.tile_pool(name="stage", bufs=2))
+        xt_banks = ctx.enter_context(tc.psum_pool(name="xt_banks", bufs=TILES))
+        banks = ctx.enter_context(tc.psum_pool(name="banks", bufs=1))
+
+        w_planes = const.tile([P, PASSES, OUT], U8, align_bytes=64)
+        nc.vector.memset(w_planes[:].bitcast(I32), 0)
+        w_words = const.tile([P, PASSES, 2 * OUT], U8, align_bytes=64)
+        lb_sb = const.tile([P, ADAPTERS, RANK], BF16)
+        lbT = const.tile([P, ADAPTERS, OUT], BF16)
+        ident_f32 = const.tile([P, P], F32)
+        make_identity(nc, ident_f32[:])
+        ident_bf16 = const.tile([P, P], BF16)
+        make_identity(nc, ident_bf16[:])
+
+        x_chunks = []
+        t_chunks = []
+
+        def load_chunk(c):
+            x_sb = resident.tile([P, TILES, IN], BF16)
+            nc.sync.dma_start(out=x_sb[:], in_=chunk_view(x_rows, c))
+            x_chunks.append(x_sb)
+            t_sb = resident.tile([P, TILES, RANK], BF16)
+            nc.sync.dma_start(out=t_sb[:], in_=chunk_view(t_rows, c))
+            t_chunks.append(t_sb)
+
+        def load_weights():
+            nc.sync.dma_start(
+                out=w_words[:].bitcast(I32), in_=W_words.rearrange("g p b -> p g b").bitcast(I32)
+            )
+            for quadrant in range(QUADRANTS):
+                nc.sync.dma_start(
+                    out=w_planes[32 * quadrant : 32 * quadrant + 4, :, :].bitcast(I32),
+                    in_=W_scales[:, 4 * quadrant : 4 * quadrant + 4, :]
+                    .rearrange("g r o -> r g o")
+                    .bitcast(I32),
+                )
+            nc.sync.dma_start(out=lb_sb[:], in_=lora_b.rearrange("a o r -> o a r"))
+
+        load_chunk(0)
+        load_weights()
+        for c in range(1, CHUNKS):
+            load_chunk(c)
+
+        quantised = []
+
+        def transpose_and_quantise(c):
+            grouped = stage.tile([P, TILES, PASSES, P, PACK], BF16, align_bytes=64)
+            codes = stage.tile([P, TILES, PASSES, P], U32, align_bytes=64)
+            planes = stage.tile([P, TILES, PASSES, P], U8, align_bytes=64)
+
+            def quantise(j):
+                nc.vector.quantize_mx(
+                    out=codes[:, j, :, :].rearrange("p g k -> p (g k)").bitcast(FP8X4),
+                    scales=planes[:, j, :, :].rearrange("p g k -> p (g k)"),
+                    in_=grouped[:, j, :, :, :].rearrange("p g k t -> p (g k t)"),
+                )
+
+            for j in range(TILES):
+                words = x_chunks[c][:, j, :].bitcast(F32)
+                xt = xt_banks.tile([P, PASSES, HALVES, P], F32)
+                for g in range(PASSES):
+                    for u in range(HALVES):
+                        columns = slice(g * WORDS_PER_PASS + u, (g + 1) * WORDS_PER_PASS, HALVES)
+                        nc.tensor.transpose(xt[:, g, u, :], words[:, columns], ident_f32[:])
+                side_by_side = xt[:].rearrange("p g u k -> p g k u")
+                if j < SCALAR_COPIES:
+                    nc.scalar.copy(out=grouped[:, j, :, :, :].bitcast(F32), in_=side_by_side)
+                else:
+                    nc.vector.tensor_copy(out=grouped[:, j, :, :, :].bitcast(F32), in_=side_by_side)
+                if j >= 1:
+                    quantise(j - 1)
+
+            tT_ps = banks.tile([P, TILES, P], BF16)
+            for j in range(TILES):
+                nc.tensor.transpose(tT_ps[:, j, :], t_chunks[c][:, j, :], ident_bf16[:])
+            tT = stage.tile([P, TILES, P], BF16)
+            nc.vector.tensor_copy(out=tT[:], in_=tT_ps[:])
+            quantise(TILES - 1)
+            quantised.append((codes, planes, tT))
+
+        def transpose_adapters():
+            lbT_ps = banks.tile([P, ADAPTERS, OUT], BF16)
+            for a in range(ADAPTERS):
+                nc.tensor.transpose(lbT_ps[:, a, :], lb_sb[:, a, :], ident_bf16[:])
+            nc.scalar.copy(out=lbT[:], in_=lbT_ps[:])
+
+        def multiply_and_store(c):
+            codes, planes, tT = quantised[c]
+            adapter = c // CHUNKS_PER_ADAPTER
+            delta_ps = banks.tile([P, TILES, OUT], F32)
+            for j in range(TILES):
+                nc.tensor.matmul(
+                    delta_ps[:, j, :], lhsT=tT[:, j, :], rhs=lbT[:, adapter, :], start=True, stop=True
+                )
+            out_sb = resident.tile([P, TILES, OUT], F32)
+            nc.scalar.copy(out=out_sb[:], in_=delta_ps[:])
+            base_ps = banks.tile([P, TILES, OUT], F32)
+            for j in range(TILES):
+                for g in range(PASSES):
+                    nc.tensor.matmul_mx(
+                        out=base_ps[:, j, :],
+                        lhsT=codes[:, j, g, :].bitcast(FP8X4),
+                        lhsT_scale=planes[:, j, g, :],
+                        rhs=w_words[:, g, :].bitcast(FP4X4),
+                        rhs_scale=w_planes[:, g, :],
+                        start=(g == 0),
+                        stop=(g == PASSES - 1),
+                    )
+            nc.vector.scalar_tensor_tensor(
+                out=out_sb[:], in0=out_sb[:], scalar=SCALING, in1=base_ps[:], op0=MULT, op1=ADD
+            )
+            nc.sync.dma_start(out=chunk_view(out_rows, c), in_=out_sb[:])
+
+        transpose_and_quantise(0)
+        transpose_adapters()
+        for c in range(1, CHUNKS):
+            transpose_and_quantise(c)
+            multiply_and_store(c - 1)
+        multiply_and_store(CHUNKS - 1)

@@ -25,7 +25,8 @@ TILES = 4
 CHUNK = TILES * P
 CHUNKS = TOKENS // CHUNK
 CHUNKS_PER_ADAPTER = SEQ // CHUNK
-SCALAR_COPIES = 3
+STRIDED_TILES = 2
+SORTED_TILES = TILES - STRIDED_TILES
 QUADRANTS = 4
 
 FLOPS = 2 * TOKENS * IN * OUT + 2 * TOKENS * RANK * OUT
@@ -88,7 +89,18 @@ def tile_linear_pa_t_kernel(tc, data, W_words, W_scales, t_lora, lora_b, out):
         for c in range(1, CHUNKS):
             load_chunk(c)
 
+        sorted_chunks = []
         quantised = []
+
+        def sort_words(c):
+            sorted_words = stage.tile([P, SORTED_TILES, PASSES, HALVES, P], F32)
+            nc.vector.tensor_copy(
+                out=sorted_words[:],
+                in_=x_chunks[c][:, STRIDED_TILES:, :]
+                .bitcast(F32)
+                .rearrange("p j (g q u) -> p j g u q", g=PASSES, u=HALVES),
+            )
+            sorted_chunks.append(sorted_words)
 
         def transpose_and_quantise(c):
             grouped = stage.tile([P, TILES, PASSES, P, PACK], BF16, align_bytes=64)
@@ -107,13 +119,15 @@ def tile_linear_pa_t_kernel(tc, data, W_words, W_scales, t_lora, lora_b, out):
                 xt = xt_banks.tile([P, PASSES, HALVES, P], F32)
                 for g in range(PASSES):
                     for u in range(HALVES):
-                        columns = slice(g * WORDS_PER_PASS + u, (g + 1) * WORDS_PER_PASS, HALVES)
-                        nc.tensor.transpose(xt[:, g, u, :], words[:, columns], ident_f32[:])
-                side_by_side = xt[:].rearrange("p g u k -> p g k u")
-                if j < SCALAR_COPIES:
-                    nc.scalar.copy(out=grouped[:, j, :, :, :].bitcast(F32), in_=side_by_side)
-                else:
-                    nc.vector.tensor_copy(out=grouped[:, j, :, :, :].bitcast(F32), in_=side_by_side)
+                        if j < STRIDED_TILES:
+                            columns = slice(g * WORDS_PER_PASS + u, (g + 1) * WORDS_PER_PASS, HALVES)
+                            half = words[:, columns]
+                        else:
+                            half = sorted_chunks[c][:, j - STRIDED_TILES, g, u, :]
+                        nc.tensor.transpose(xt[:, g, u, :], half, ident_f32[:])
+                nc.scalar.copy(
+                    out=grouped[:, j, :, :, :].bitcast(F32), in_=xt[:].rearrange("p g u k -> p g k u")
+                )
                 if j >= 1:
                     quantise(j - 1)
 
@@ -158,9 +172,13 @@ def tile_linear_pa_t_kernel(tc, data, W_words, W_scales, t_lora, lora_b, out):
             )
             nc.sync.dma_start(out=chunk_view(out_rows, c), in_=out_sb[:])
 
-        transpose_and_quantise(0)
-        transpose_adapters()
-        for c in range(1, CHUNKS):
-            transpose_and_quantise(c)
-            multiply_and_store(c - 1)
-        multiply_and_store(CHUNKS - 1)
+        sort_words(0)
+        for c in range(CHUNKS + 1):
+            if c + 1 < CHUNKS:
+                sort_words(c + 1)
+            if c < CHUNKS:
+                transpose_and_quantise(c)
+            if c == 0:
+                transpose_adapters()
+            else:
+                multiply_and_store(c - 1)

@@ -25,7 +25,7 @@ TILES = 4
 CHUNK = TILES * P
 CHUNKS = TOKENS // CHUNK
 CHUNKS_PER_ADAPTER = SEQ // CHUNK
-STRIDED_TILES = 2
+STRIDED_TILES = 1
 SORTED_TILES = TILES - STRIDED_TILES
 QUADRANTS = 4
 

@@ -25,8 +25,9 @@ TILES = 4
 CHUNK = TILES * P
 CHUNKS = TOKENS // CHUNK
 CHUNKS_PER_ADAPTER = SEQ // CHUNK
-STRIDED_TILES = 1
-SORTED_TILES = TILES - STRIDED_TILES
+HALF = TILES // 2
+FIRST_HALF = (0, 1)
+SECOND_HALF = (2, 3)
 QUADRANTS = 4
 
 FLOPS = 2 * TOKENS * IN * OUT + 2 * TOKENS * RANK * OUT
@@ -89,55 +90,70 @@ def tile_linear_pa_t_kernel(tc, data, W_words, W_scales, t_lora, lora_b, out):
         for c in range(1, CHUNKS):
             load_chunk(c)
 
-        sorted_chunks = []
-        quantised = []
+        tiles_of = {}
+
+        def exists(c):
+            return 0 <= c < CHUNKS
 
         def sort_words(c):
-            sorted_words = stage.tile([P, SORTED_TILES, PASSES, HALVES, P], F32)
+            if not exists(c):
+                return
+            sorted_words = stage.tile([P, HALF, PASSES, HALVES, P], F32)
             nc.vector.tensor_copy(
                 out=sorted_words[:],
-                in_=x_chunks[c][:, STRIDED_TILES:, :]
+                in_=x_chunks[c][:, SECOND_HALF[0] :, :]
                 .bitcast(F32)
                 .rearrange("p j (g q u) -> p j g u q", g=PASSES, u=HALVES),
             )
-            sorted_chunks.append(sorted_words)
+            tiles_of[c] = {"sorted_words": sorted_words}
 
-        def transpose_and_quantise(c):
-            grouped = stage.tile([P, TILES, PASSES, P, PACK], BF16, align_bytes=64)
-            codes = stage.tile([P, TILES, PASSES, P], U32, align_bytes=64)
-            planes = stage.tile([P, TILES, PASSES, P], U8, align_bytes=64)
-
-            def quantise(j):
-                nc.vector.quantize_mx(
-                    out=codes[:, j, :, :].rearrange("p g k -> p (g k)").bitcast(FP8X4),
-                    scales=planes[:, j, :, :].rearrange("p g k -> p (g k)"),
-                    in_=grouped[:, j, :, :, :].rearrange("p g k t -> p (g k t)"),
-                )
-
-            for j in range(TILES):
-                words = x_chunks[c][:, j, :].bitcast(F32)
+        def transpose_words(c, half):
+            if not exists(c):
+                return
+            mine = tiles_of[c]
+            if half == FIRST_HALF:
+                grouped = stage.tile([P, TILES, PASSES, P, PACK], BF16, align_bytes=64)
+                mine["grouped"] = grouped
+            for j in half:
                 xt = xt_banks.tile([P, PASSES, HALVES, P], F32)
                 for g in range(PASSES):
                     for u in range(HALVES):
-                        if j < STRIDED_TILES:
+                        if half == FIRST_HALF:
                             columns = slice(g * WORDS_PER_PASS + u, (g + 1) * WORDS_PER_PASS, HALVES)
-                            half = words[:, columns]
+                            words = x_chunks[c][:, j, :].bitcast(F32)[:, columns]
                         else:
-                            half = sorted_chunks[c][:, j - STRIDED_TILES, g, u, :]
-                        nc.tensor.transpose(xt[:, g, u, :], half, ident_f32[:])
+                            words = mine["sorted_words"][:, j - SECOND_HALF[0], g, u, :]
+                        nc.tensor.transpose(xt[:, g, u, :], words, ident_f32[:])
                 nc.scalar.copy(
-                    out=grouped[:, j, :, :, :].bitcast(F32), in_=xt[:].rearrange("p g u k -> p g k u")
+                    out=mine["grouped"][:, j, :, :, :].bitcast(F32),
+                    in_=xt[:].rearrange("p g u k -> p g k u"),
                 )
-                if j >= 1:
-                    quantise(j - 1)
 
+        def quantise(c, half):
+            if not exists(c):
+                return
+            mine = tiles_of[c]
+            if half == FIRST_HALF:
+                codes = stage.tile([P, TILES, PASSES, P], U32, align_bytes=64)
+                planes = stage.tile([P, TILES, PASSES, P], U8, align_bytes=64)
+                mine["codes"] = codes
+                mine["planes"] = planes
+            both = slice(half[0], half[0] + HALF)
+            nc.vector.quantize_mx(
+                out=mine["codes"][:, both, :, :].rearrange("p j g k -> p (j g k)").bitcast(FP8X4),
+                scales=mine["planes"][:, both, :, :].rearrange("p j g k -> p (j g k)"),
+                in_=mine["grouped"][:, both, :, :, :].rearrange("p j g k t -> p (j g k t)"),
+            )
+
+        def transpose_t(c):
+            if not exists(c):
+                return
             tT_ps = banks.tile([P, TILES, P], BF16)
             for j in range(TILES):
                 nc.tensor.transpose(tT_ps[:, j, :], t_chunks[c][:, j, :], ident_bf16[:])
             tT = stage.tile([P, TILES, P], BF16)
             nc.vector.tensor_copy(out=tT[:], in_=tT_ps[:])
-            quantise(TILES - 1)
-            quantised.append((codes, planes, tT))
+            tiles_of[c]["tT"] = tT
 
         def transpose_adapters():
             lbT_ps = banks.tile([P, ADAPTERS, OUT], BF16)
@@ -145,23 +161,35 @@ def tile_linear_pa_t_kernel(tc, data, W_words, W_scales, t_lora, lora_b, out):
                 nc.tensor.transpose(lbT_ps[:, a, :], lb_sb[:, a, :], ident_bf16[:])
             nc.scalar.copy(out=lbT[:], in_=lbT_ps[:])
 
-        def multiply_and_store(c):
-            codes, planes, tT = quantised[c]
-            adapter = c // CHUNKS_PER_ADAPTER
-            delta_ps = banks.tile([P, TILES, OUT], F32)
-            for j in range(TILES):
+        def adapter_product(c, half):
+            if not exists(c):
+                return
+            mine = tiles_of[c]
+            if half == FIRST_HALF:
+                delta_ps = banks.tile([P, TILES, OUT], F32)
+                mine["delta_ps"] = delta_ps
+            for j in half:
                 nc.tensor.matmul(
-                    delta_ps[:, j, :], lhsT=tT[:, j, :], rhs=lbT[:, adapter, :], start=True, stop=True
+                    mine["delta_ps"][:, j, :],
+                    lhsT=mine["tT"][:, j, :],
+                    rhs=lbT[:, c // CHUNKS_PER_ADAPTER, :],
+                    start=True,
+                    stop=True,
                 )
+
+        def base_product_and_store(c):
+            if not exists(c):
+                return
+            mine = tiles_of[c]
             out_sb = resident.tile([P, TILES, OUT], F32)
-            nc.scalar.copy(out=out_sb[:], in_=delta_ps[:])
+            nc.scalar.copy(out=out_sb[:], in_=mine["delta_ps"][:])
             base_ps = banks.tile([P, TILES, OUT], F32)
             for j in range(TILES):
                 for g in range(PASSES):
                     nc.tensor.matmul_mx(
                         out=base_ps[:, j, :],
-                        lhsT=codes[:, j, g, :].bitcast(FP8X4),
-                        lhsT_scale=planes[:, j, g, :],
+                        lhsT=mine["codes"][:, j, g, :].bitcast(FP8X4),
+                        lhsT_scale=mine["planes"][:, j, g, :],
                         rhs=w_words[:, g, :].bitcast(FP4X4),
                         rhs_scale=w_planes[:, g, :],
                         start=(g == 0),
@@ -172,13 +200,19 @@ def tile_linear_pa_t_kernel(tc, data, W_words, W_scales, t_lora, lora_b, out):
             )
             nc.sync.dma_start(out=chunk_view(out_rows, c), in_=out_sb[:])
 
+        def one_round(c):
+            sort_words(c + 1)
+            transpose_words(c, FIRST_HALF)
+            quantise(c, FIRST_HALF)
+            adapter_product(c - 1, FIRST_HALF)
+            transpose_words(c, SECOND_HALF)
+            transpose_t(c)
+            quantise(c, SECOND_HALF)
+            adapter_product(c - 1, SECOND_HALF)
+            base_product_and_store(c - 1)
+
         sort_words(0)
-        for c in range(CHUNKS + 1):
-            if c + 1 < CHUNKS:
-                sort_words(c + 1)
-            if c < CHUNKS:
-                transpose_and_quantise(c)
-            if c == 0:
-                transpose_adapters()
-            else:
-                multiply_and_store(c - 1)
+        one_round(0)
+        transpose_adapters()
+        for c in range(1, CHUNKS + 1):
+            one_round(c)

@@ -33,6 +33,21 @@ QUADRANTS = 4
 FLOPS = 2 * TOKENS * IN * OUT + 2 * TOKENS * RANK * OUT
 
 
+CFG = dict(
+    head_loads=("x0", "t0", "W", "s", "lb"),
+    lb_rows="o",
+    unsorted_chunks=0,
+    vector_sorts=(2, 3),
+    gpsimd_sorts=(),
+    sort_place="first",
+    pe_order="middle",
+    delta_bufs=1,
+    t_copy="vector",
+    vector_copies=(),
+    tail="halves",
+)
+
+
 def chunk_view(rows, c):
     return rows[c * CHUNK : (c + 1) * CHUNK, :].rearrange("(p j) w -> p j w", j=TILES)
 
@@ -61,84 +76,130 @@ def tile_linear_pa_t_kernel(tc, data, W_words, W_scales, t_lora, lora_b, out):
         ident_bf16 = const.tile([P, P], BF16)
         make_identity(nc, ident_bf16[:])
 
-        x_chunks = []
-        t_chunks = []
+        x_chunks = {}
+        t_chunks = {}
 
-        def load_chunk(c):
-            x_sb = resident.tile([P, TILES, IN], BF16)
-            nc.sync.dma_start(out=x_sb[:], in_=chunk_view(x_rows, c))
-            x_chunks.append(x_sb)
-            t_sb = resident.tile([P, TILES, RANK], BF16)
-            nc.sync.dma_start(out=t_sb[:], in_=chunk_view(t_rows, c))
-            t_chunks.append(t_sb)
+        def x_tile(c):
+            if c not in x_chunks:
+                x_sb = resident.tile([P, TILES, IN], BF16)
+                x_chunks[c] = x_sb
+            return x_chunks[c]
 
-        def load_weights():
-            nc.sync.dma_start(
-                out=w_words[:].bitcast(I32), in_=W_words.rearrange("g p b -> p g b").bitcast(I32)
-            )
-            for quadrant in range(QUADRANTS):
+        def load(what):
+            if what == "W":
                 nc.sync.dma_start(
-                    out=w_planes[32 * quadrant : 32 * quadrant + 4, :, :].bitcast(I32),
-                    in_=W_scales[:, 4 * quadrant : 4 * quadrant + 4, :]
-                    .rearrange("g r o -> r g o")
-                    .bitcast(I32),
+                    out=w_words[:].bitcast(I32), in_=W_words.rearrange("g p b -> p g b").bitcast(I32)
                 )
-            nc.sync.dma_start(out=lb_sb[:], in_=lora_b.rearrange("a o r -> o a r"))
+            elif what == "s":
+                for quadrant in range(QUADRANTS):
+                    nc.sync.dma_start(
+                        out=w_planes[32 * quadrant : 32 * quadrant + 4, :, :].bitcast(I32),
+                        in_=W_scales[:, 4 * quadrant : 4 * quadrant + 4, :]
+                        .rearrange("g r o -> r g o")
+                        .bitcast(I32),
+                    )
+            elif what == "lb":
+                if CFG["lb_rows"] == "o":
+                    nc.sync.dma_start(out=lb_sb[:], in_=lora_b.rearrange("a o r -> o a r"))
+                else:
+                    nc.sync.dma_start(
+                        out=lb_sb[:], in_=lora_b.rearrange("a (h i) r -> (a h) i r", i=ADAPTERS)
+                    )
+            elif what.startswith("t"):
+                c = int(what[1:])
+                t_sb = resident.tile([P, TILES, RANK], BF16)
+                nc.sync.dma_start(out=t_sb[:], in_=chunk_view(t_rows, c))
+                t_chunks[c] = t_sb
+            elif "." in what:
+                c = int(what[1:].split(".")[0])
+                lo, hi = what.split(".")[1].split("-")
+                nc.sync.dma_start(
+                    out=x_tile(c)[:, int(lo) : int(hi), :], in_=chunk_view(x_rows, c)[:, int(lo) : int(hi), :]
+                )
+            else:
+                c = int(what[1:])
+                nc.sync.dma_start(out=x_tile(c)[:], in_=chunk_view(x_rows, c))
 
-        load_chunk(0)
-        load_weights()
-        for c in range(1, CHUNKS):
-            load_chunk(c)
+        for what in CFG["head_loads"]:
+            load(what)
+        for c in range(CHUNKS):
+            if c not in x_chunks:
+                load("x%d" % c)
+            if c not in t_chunks:
+                load("t%d" % c)
 
         tiles_of = {}
 
         def exists(c):
             return 0 <= c < CHUNKS
 
-        def sort_words(c):
-            if not exists(c):
-                return
-            sorted_words = stage.tile([P, HALF, PASSES, HALVES, P], F32)
-            nc.vector.tensor_copy(
-                out=sorted_words[:],
-                in_=x_chunks[c][:, SECOND_HALF[0] :, :]
-                .bitcast(F32)
-                .rearrange("p j (g q u) -> p j g u q", g=PASSES, u=HALVES),
-            )
-            tiles_of[c] = {"sorted_words": sorted_words}
+        def mine_of(c):
+            return tiles_of.setdefault(c, {})
 
-        def transpose_words(c, half):
+        def sorted_tiles(c):
+            if c < CFG["unsorted_chunks"]:
+                return ()
+            return tuple(sorted(CFG["vector_sorts"] + CFG["gpsimd_sorts"]))
+
+        def sort_words(c, who):
+            if not exists(c) or c < CFG["unsorted_chunks"]:
+                return
+            mine = mine_of(c)
+            if "sorted_words" not in mine:
+                sorted_words = stage.tile([P, TILES, PASSES, HALVES, P], F32)
+                mine["sorted_words"] = sorted_words
+            tiles = CFG["vector_sorts"] if who == "vector" else CFG["gpsimd_sorts"]
+            if not tiles:
+                return
+            if who == "vector":
+                lo, hi = tiles[0], tiles[-1] + 1
+                nc.vector.tensor_copy(
+                    out=mine["sorted_words"][:, lo:hi],
+                    in_=x_chunks[c][:, lo:hi, :].bitcast(F32).rearrange("p j (g q u) -> p j g u q", g=PASSES, u=HALVES),
+                )
+            else:
+                for j in tiles:
+                    nc.gpsimd.tensor_copy(
+                        out=mine["sorted_words"][:, j],
+                        in_=x_chunks[c][:, j, :].bitcast(F32).rearrange("p (g q u) -> p g u q", g=PASSES, u=HALVES),
+                    )
+
+        def transpose_words(c, tiles):
             if not exists(c):
                 return
-            mine = tiles_of[c]
-            if half == FIRST_HALF:
+            mine = mine_of(c)
+            if "grouped" not in mine:
                 grouped = stage.tile([P, TILES, PASSES, P, PACK], BF16, align_bytes=64)
                 mine["grouped"] = grouped
-            for j in half:
-                xt = xt_banks.tile([P, PASSES, HALVES, P], F32)
+            for j in tiles:
+                xt = xt_banks.tile([P, PASSES, HALVES, P], F32, tag="xt")
                 for g in range(PASSES):
                     for u in range(HALVES):
-                        if half == FIRST_HALF:
+                        if j in sorted_tiles(c):
+                            words = mine["sorted_words"][:, j, g, u, :]
+                        else:
                             columns = slice(g * WORDS_PER_PASS + u, (g + 1) * WORDS_PER_PASS, HALVES)
                             words = x_chunks[c][:, j, :].bitcast(F32)[:, columns]
-                        else:
-                            words = mine["sorted_words"][:, j - SECOND_HALF[0], g, u, :]
                         nc.tensor.transpose(xt[:, g, u, :], words, ident_f32[:])
-                nc.scalar.copy(
-                    out=mine["grouped"][:, j, :, :, :].bitcast(F32),
-                    in_=xt[:].rearrange("p g u k -> p g k u"),
-                )
+                if j in CFG["vector_copies"]:
+                    nc.vector.tensor_copy(
+                        out=mine["grouped"][:, j, :, :, :].bitcast(F32), in_=xt[:].rearrange("p g u k -> p g k u")
+                    )
+                else:
+                    nc.scalar.copy(
+                        out=mine["grouped"][:, j, :, :, :].bitcast(F32), in_=xt[:].rearrange("p g u k -> p g k u")
+                    )
 
-        def quantise(c, half):
+        def quantise(c, tiles):
             if not exists(c):
                 return
-            mine = tiles_of[c]
-            if half == FIRST_HALF:
+            mine = mine_of(c)
+            if "codes" not in mine:
                 codes = stage.tile([P, TILES, PASSES, P], U32, align_bytes=64)
                 planes = stage.tile([P, TILES, PASSES, P], U8, align_bytes=64)
                 mine["codes"] = codes
                 mine["planes"] = planes
-            both = slice(half[0], half[0] + HALF)
+            both = slice(tiles[0], tiles[-1] + 1)
             nc.vector.quantize_mx(
                 out=mine["codes"][:, both, :, :].rearrange("p j g k -> p (j g k)").bitcast(FP8X4),
                 scales=mine["planes"][:, both, :, :].rearrange("p j g k -> p (j g k)"),
@@ -148,27 +209,36 @@ def tile_linear_pa_t_kernel(tc, data, W_words, W_scales, t_lora, lora_b, out):
         def transpose_t(c):
             if not exists(c):
                 return
-            tT_ps = banks.tile([P, TILES, P], BF16)
+            tT_ps = banks.tile([P, ADAPTERS, P], BF16, tag="bf16_bank")
             for j in range(TILES):
                 nc.tensor.transpose(tT_ps[:, j, :], t_chunks[c][:, j, :], ident_bf16[:])
             tT = stage.tile([P, TILES, P], BF16)
-            nc.vector.tensor_copy(out=tT[:], in_=tT_ps[:])
-            tiles_of[c]["tT"] = tT
+            if CFG["t_copy"] == "vector":
+                nc.vector.tensor_copy(out=tT[:], in_=tT_ps[:, :TILES, :])
+            else:
+                nc.scalar.copy(out=tT[:], in_=tT_ps[:, :TILES, :])
+            mine_of(c)["tT"] = tT
 
         def transpose_adapters():
-            lbT_ps = banks.tile([P, ADAPTERS, OUT], BF16)
+            lbT_ps = banks.tile([P, ADAPTERS, OUT], BF16, tag="bf16_bank")
             for a in range(ADAPTERS):
                 nc.tensor.transpose(lbT_ps[:, a, :], lb_sb[:, a, :], ident_bf16[:])
-            nc.scalar.copy(out=lbT[:], in_=lbT_ps[:])
+            if CFG["lb_rows"] == "o":
+                nc.scalar.copy(out=lbT[:], in_=lbT_ps[:])
+            else:
+                nc.scalar.copy(
+                    out=lbT[:].rearrange("r a (h i) -> r a h i", i=ADAPTERS),
+                    in_=lbT_ps[:].rearrange("r i (a h) -> r a h i", a=ADAPTERS),
+                )
 
-        def adapter_product(c, half):
+        def adapter_product(c, tiles):
             if not exists(c):
                 return
-            mine = tiles_of[c]
-            if half == FIRST_HALF:
-                delta_ps = banks.tile([P, TILES, OUT], F32)
+            mine = mine_of(c)
+            if "delta_ps" not in mine:
+                delta_ps = banks.tile([P, TILES, OUT], F32, bufs=CFG["delta_bufs"])
                 mine["delta_ps"] = delta_ps
-            for j in half:
+            for j in tiles:
                 nc.tensor.matmul(
                     mine["delta_ps"][:, j, :],
                     lhsT=mine["tT"][:, j, :],
@@ -180,38 +250,58 @@ def tile_linear_pa_t_kernel(tc, data, W_words, W_scales, t_lora, lora_b, out):
         def base_product_and_store(c):
             if not exists(c):
                 return
-            mine = tiles_of[c]
+            mine = mine_of(c)
             out_sb = resident.tile([P, TILES, OUT], F32)
             nc.scalar.copy(out=out_sb[:], in_=mine["delta_ps"][:])
-            base_ps = banks.tile([P, TILES, OUT], F32)
-            for j in range(TILES):
-                for g in range(PASSES):
-                    nc.tensor.matmul_mx(
-                        out=base_ps[:, j, :],
-                        lhsT=mine["codes"][:, j, g, :].bitcast(FP8X4),
-                        lhsT_scale=mine["planes"][:, j, g, :],
-                        rhs=w_words[:, g, :].bitcast(FP4X4),
-                        rhs_scale=w_planes[:, g, :],
-                        start=(g == 0),
-                        stop=(g == PASSES - 1),
-                    )
-            nc.vector.scalar_tensor_tensor(
-                out=out_sb[:], in0=out_sb[:], scalar=SCALING, in1=base_ps[:], op0=MULT, op1=ADD
-            )
-            nc.sync.dma_start(out=chunk_view(out_rows, c), in_=out_sb[:])
+            if c == CHUNKS - 1 and CFG["tail"] == "halves":
+                groups = (FIRST_HALF, SECOND_HALF)
+            else:
+                groups = (FIRST_HALF + SECOND_HALF,)
+            for n, group in enumerate(groups):
+                if n == 0:
+                    base_ps = banks.tile([P, TILES, OUT], F32)
+                else:
+                    base_ps = xt_banks.tile([P, TILES, OUT], F32, tag="xt")
+                for j in group:
+                    for g in range(PASSES):
+                        nc.tensor.matmul_mx(
+                            out=base_ps[:, j, :],
+                            lhsT=mine["codes"][:, j, g, :].bitcast(FP8X4),
+                            lhsT_scale=mine["planes"][:, j, g, :],
+                            rhs=w_words[:, g, :].bitcast(FP4X4),
+                            rhs_scale=w_planes[:, g, :],
+                            start=(g == 0),
+                            stop=(g == PASSES - 1),
+                        )
+                these = slice(group[0], group[-1] + 1)
+                nc.vector.scalar_tensor_tensor(
+                    out=out_sb[:, these, :], in0=out_sb[:, these, :], scalar=SCALING, in1=base_ps[:, these, :], op0=MULT, op1=ADD
+                )
+                nc.sync.dma_start(out=chunk_view(out_rows, c)[:, these, :], in_=out_sb[:, these, :])
 
         def one_round(c):
-            sort_words(c + 1)
+            place = CFG["sort_place"]
+            sort_words(c + 1, "gpsimd")
+            if place == "first":
+                sort_words(c + 1, "vector")
+            if CFG["pe_order"] == "after_mx":
+                adapter_product(c - 1, FIRST_HALF)
             transpose_words(c, FIRST_HALF)
             quantise(c, FIRST_HALF)
-            adapter_product(c - 1, FIRST_HALF)
+            if place == "mid":
+                sort_words(c + 1, "vector")
+            if CFG["pe_order"] == "middle":
+                adapter_product(c - 1, FIRST_HALF)
             transpose_words(c, SECOND_HALF)
             transpose_t(c)
             quantise(c, SECOND_HALF)
+            if place == "late":
+                sort_words(c + 1, "vector")
             adapter_product(c - 1, SECOND_HALF)
             base_product_and_store(c - 1)
 
-        sort_words(0)
+        sort_words(0, "gpsimd")
+        sort_words(0, "vector")
         one_round(0)
         transpose_adapters()
         for c in range(1, CHUNKS + 1):

@@ -34,8 +34,8 @@ FLOPS = 2 * TOKENS * IN * OUT + 2 * TOKENS * RANK * OUT
 
 
 CFG = dict(
-    head_loads=("x0", "t0", "W", "s", "lb"),
-    lb_rows="o",
+    head_loads=("x0", "t0", "lb", "x1", "W", "s", "t1"),
+    lb_rows="ao",
     unsorted_chunks=0,
     vector_sorts=(2, 3),
     gpsimd_sorts=(),
@@ -209,18 +209,18 @@ def tile_linear_pa_t_kernel(tc, data, W_words, W_scales, t_lora, lora_b, out):
         def transpose_t(c):
             if not exists(c):
                 return
-            tT_ps = banks.tile([P, ADAPTERS, P], BF16, tag="bf16_bank")
+            tT_ps = banks.tile([P, TILES, P], BF16)
             for j in range(TILES):
                 nc.tensor.transpose(tT_ps[:, j, :], t_chunks[c][:, j, :], ident_bf16[:])
             tT = stage.tile([P, TILES, P], BF16)
             if CFG["t_copy"] == "vector":
-                nc.vector.tensor_copy(out=tT[:], in_=tT_ps[:, :TILES, :])
+                nc.vector.tensor_copy(out=tT[:], in_=tT_ps[:])
             else:
-                nc.scalar.copy(out=tT[:], in_=tT_ps[:, :TILES, :])
+                nc.scalar.copy(out=tT[:], in_=tT_ps[:])
             mine_of(c)["tT"] = tT
 
         def transpose_adapters():
-            lbT_ps = banks.tile([P, ADAPTERS, OUT], BF16, tag="bf16_bank")
+            lbT_ps = xt_banks.tile([P, ADAPTERS, OUT], BF16, tag="xt")
             for a in range(ADAPTERS):
                 nc.tensor.transpose(lbT_ps[:, a, :], lb_sb[:, a, :], ident_bf16[:])
             if CFG["lb_rows"] == "o":

@@ -41,10 +41,10 @@ CFG = dict(
     gpsimd_sorts=(),
     sort_place="first",
     pe_order="middle",
-    delta_bufs=1,
+    delta_bufs=2,
     t_copy="vector",
     vector_copies=(),
-    tail="halves",
+    tail="fine",
 )
 
 
@@ -255,6 +255,8 @@ def tile_linear_pa_t_kernel(tc, data, W_words, W_scales, t_lora, lora_b, out):
             nc.scalar.copy(out=out_sb[:], in_=mine["delta_ps"][:])
             if c == CHUNKS - 1 and CFG["tail"] == "halves":
                 groups = (FIRST_HALF, SECOND_HALF)
+            elif c == CHUNKS - 1 and CFG["tail"] == "fine":
+                groups = (FIRST_HALF, SECOND_HALF[:1], SECOND_HALF[1:])
             else:
                 groups = (FIRST_HALF + SECOND_HALF,)
             for n, group in enumerate(groups):
@@ -294,7 +296,11 @@ def tile_linear_pa_t_kernel(tc, data, W_words, W_scales, t_lora, lora_b, out):
                 adapter_product(c - 1, FIRST_HALF)
             transpose_words(c, SECOND_HALF)
             transpose_t(c)
-            quantise(c, SECOND_HALF)
+            if c == CHUNKS - 1 and CFG["tail"] == "fine":
+                quantise(c, SECOND_HALF[:1])
+                quantise(c, SECOND_HALF[1:])
+            else:
+                quantise(c, SECOND_HALF)
             if place == "late":
                 sort_words(c + 1, "vector")
             adapter_product(c - 1, SECOND_HALF)

@@ -260,7 +260,7 @@ def tile_linear_pa_t_kernel(tc, data, W_words, W_scales, t_lora, lora_b, out):
             else:
                 groups = (FIRST_HALF + SECOND_HALF,)
             for n, group in enumerate(groups):
-                if n == 0:
+                if len(groups) == 1:
                     base_ps = banks.tile([P, TILES, OUT], F32)
                 else:
                     base_ps = xt_banks.tile([P, TILES, OUT], F32, tag="xt")

@@ -24,32 +24,34 @@ WORDS_PER_PASS = P * HALVES
 TILES = 4
 CHUNK = TILES * P
 CHUNKS = TOKENS // CHUNK
+LAST = CHUNKS - 1
 CHUNKS_PER_ADAPTER = SEQ // CHUNK
-HALF = TILES // 2
 FIRST_HALF = (0, 1)
 SECOND_HALF = (2, 3)
 QUADRANTS = 4
+ROWS_PER_PARTITION = ADAPTERS * OUT // P
 
 FLOPS = 2 * TOKENS * IN * OUT + 2 * TOKENS * RANK * OUT
 
 
-CFG = dict(
-    head_loads=("x0", "t0", "lb", "x1", "W", "s", "t1"),
-    lb_rows="ao",
-    unsorted_chunks=0,
-    vector_sorts=(2, 3),
-    gpsimd_sorts=(),
-    sort_place="first",
-    pe_order="middle",
-    delta_bufs=2,
-    t_copy="vector",
-    vector_copies=(),
-    tail="fine",
-)
-
-
 def chunk_view(rows, c):
     return rows[c * CHUNK : (c + 1) * CHUNK, :].rearrange("(p j) w -> p j w", j=TILES)
+
+
+def span(tiles):
+    return slice(tiles[0], tiles[-1] + 1)
+
+
+def quantise_groups(c):
+    if c == LAST:
+        return (FIRST_HALF, SECOND_HALF[:1], SECOND_HALF[1:])
+    return (FIRST_HALF, SECOND_HALF)
+
+
+def product_groups(c):
+    if c == LAST:
+        return quantise_groups(c)
+    return (FIRST_HALF + SECOND_HALF,)
 
 
 def tile_linear_pa_t_kernel(tc, data, W_words, W_scales, t_lora, lora_b, out):
@@ -63,147 +65,111 @@ def tile_linear_pa_t_kernel(tc, data, W_words, W_scales, t_lora, lora_b, out):
         const = ctx.enter_context(tc.tile_pool(name="const", bufs=1))
         resident = ctx.enter_context(tc.tile_pool(name="resident", bufs=CHUNKS))
         stage = ctx.enter_context(tc.tile_pool(name="stage", bufs=2))
-        xt_banks = ctx.enter_context(tc.psum_pool(name="xt_banks", bufs=TILES))
+        word_banks = ctx.enter_context(tc.psum_pool(name="word_banks", bufs=TILES))
         banks = ctx.enter_context(tc.psum_pool(name="banks", bufs=1))
 
         w_planes = const.tile([P, PASSES, OUT], U8, align_bytes=64)
         nc.vector.memset(w_planes[:].bitcast(I32), 0)
         w_words = const.tile([P, PASSES, 2 * OUT], U8, align_bytes=64)
-        lb_sb = const.tile([P, ADAPTERS, RANK], BF16)
+        lb_sb = const.tile([P, ROWS_PER_PARTITION, RANK], BF16)
         lbT = const.tile([P, ADAPTERS, OUT], BF16)
         ident_f32 = const.tile([P, P], F32)
         make_identity(nc, ident_f32[:])
         ident_bf16 = const.tile([P, P], BF16)
         make_identity(nc, ident_bf16[:])
 
-        x_chunks = {}
-        t_chunks = {}
+        x_chunks = []
+        t_chunks = []
 
-        def x_tile(c):
-            if c not in x_chunks:
-                x_sb = resident.tile([P, TILES, IN], BF16)
-                x_chunks[c] = x_sb
-            return x_chunks[c]
+        def load_x(c):
+            x_sb = resident.tile([P, TILES, IN], BF16)
+            nc.sync.dma_start(out=x_sb[:], in_=chunk_view(x_rows, c))
+            x_chunks.append(x_sb)
 
-        def load(what):
-            if what == "W":
+        def load_t(c):
+            t_sb = resident.tile([P, TILES, RANK], BF16)
+            nc.sync.dma_start(out=t_sb[:], in_=chunk_view(t_rows, c))
+            t_chunks.append(t_sb)
+
+        def load_adapters():
+            nc.sync.dma_start(
+                out=lb_sb[:], in_=lora_b.rearrange("a (h i) r -> (a h) i r", i=ROWS_PER_PARTITION)
+            )
+
+        def load_weights():
+            nc.sync.dma_start(
+                out=w_words[:].bitcast(I32), in_=W_words.rearrange("g p b -> p g b").bitcast(I32)
+            )
+            for quadrant in range(QUADRANTS):
                 nc.sync.dma_start(
-                    out=w_words[:].bitcast(I32), in_=W_words.rearrange("g p b -> p g b").bitcast(I32)
+                    out=w_planes[32 * quadrant : 32 * quadrant + 4, :, :].bitcast(I32),
+                    in_=W_scales[:, 4 * quadrant : 4 * quadrant + 4, :]
+                    .rearrange("g r o -> r g o")
+                    .bitcast(I32),
                 )
-            elif what == "s":
-                for quadrant in range(QUADRANTS):
-                    nc.sync.dma_start(
-                        out=w_planes[32 * quadrant : 32 * quadrant + 4, :, :].bitcast(I32),
-                        in_=W_scales[:, 4 * quadrant : 4 * quadrant + 4, :]
-                        .rearrange("g r o -> r g o")
-                        .bitcast(I32),
-                    )
-            elif what == "lb":
-                if CFG["lb_rows"] == "o":
-                    nc.sync.dma_start(out=lb_sb[:], in_=lora_b.rearrange("a o r -> o a r"))
-                else:
-                    nc.sync.dma_start(
-                        out=lb_sb[:], in_=lora_b.rearrange("a (h i) r -> (a h) i r", i=ADAPTERS)
-                    )
-            elif what.startswith("t"):
-                c = int(what[1:])
-                t_sb = resident.tile([P, TILES, RANK], BF16)
-                nc.sync.dma_start(out=t_sb[:], in_=chunk_view(t_rows, c))
-                t_chunks[c] = t_sb
-            elif "." in what:
-                c = int(what[1:].split(".")[0])
-                lo, hi = what.split(".")[1].split("-")
-                nc.sync.dma_start(
-                    out=x_tile(c)[:, int(lo) : int(hi), :], in_=chunk_view(x_rows, c)[:, int(lo) : int(hi), :]
-                )
-            else:
-                c = int(what[1:])
-                nc.sync.dma_start(out=x_tile(c)[:], in_=chunk_view(x_rows, c))
 
-        for what in CFG["head_loads"]:
-            load(what)
-        for c in range(CHUNKS):
-            if c not in x_chunks:
-                load("x%d" % c)
-            if c not in t_chunks:
-                load("t%d" % c)
+        load_x(0)
+        load_t(0)
+        load_adapters()
+        load_x(1)
+        load_weights()
+        load_t(1)
+        for c in range(2, CHUNKS):
+            load_x(c)
+            load_t(c)
 
-        tiles_of = {}
+        buffers_of = {}
 
         def exists(c):
             return 0 <= c < CHUNKS
 
-        def mine_of(c):
-            return tiles_of.setdefault(c, {})
-
-        def sorted_tiles(c):
-            if c < CFG["unsorted_chunks"]:
-                return ()
-            return tuple(sorted(CFG["vector_sorts"] + CFG["gpsimd_sorts"]))
-
-        def sort_words(c, who):
-            if not exists(c) or c < CFG["unsorted_chunks"]:
-                return
-            mine = mine_of(c)
-            if "sorted_words" not in mine:
-                sorted_words = stage.tile([P, TILES, PASSES, HALVES, P], F32)
-                mine["sorted_words"] = sorted_words
-            tiles = CFG["vector_sorts"] if who == "vector" else CFG["gpsimd_sorts"]
-            if not tiles:
-                return
-            if who == "vector":
-                lo, hi = tiles[0], tiles[-1] + 1
-                nc.vector.tensor_copy(
-                    out=mine["sorted_words"][:, lo:hi],
-                    in_=x_chunks[c][:, lo:hi, :].bitcast(F32).rearrange("p j (g q u) -> p j g u q", g=PASSES, u=HALVES),
-                )
-            else:
-                for j in tiles:
-                    nc.gpsimd.tensor_copy(
-                        out=mine["sorted_words"][:, j],
-                        in_=x_chunks[c][:, j, :].bitcast(F32).rearrange("p (g q u) -> p g u q", g=PASSES, u=HALVES),
-                    )
-
-        def transpose_words(c, tiles):
+        def sort_words(c):
             if not exists(c):
                 return
-            mine = mine_of(c)
-            if "grouped" not in mine:
+            sorted_words = stage.tile([P, len(SECOND_HALF), PASSES, HALVES, P], F32)
+            nc.vector.tensor_copy(
+                out=sorted_words[:],
+                in_=x_chunks[c][:, span(SECOND_HALF), :]
+                .bitcast(F32)
+                .rearrange("p j (g q u) -> p j g u q", g=PASSES, u=HALVES),
+            )
+            buffers_of[c] = {"sorted_words": sorted_words}
+
+        def transpose_words(c, half):
+            if not exists(c):
+                return
+            mine = buffers_of[c]
+            if half == FIRST_HALF:
                 grouped = stage.tile([P, TILES, PASSES, P, PACK], BF16, align_bytes=64)
                 mine["grouped"] = grouped
-            for j in tiles:
-                xt = xt_banks.tile([P, PASSES, HALVES, P], F32, tag="xt")
+            for j in half:
+                xt = word_banks.tile([P, PASSES, HALVES, P], F32, tag="words")
                 for g in range(PASSES):
                     for u in range(HALVES):
-                        if j in sorted_tiles(c):
-                            words = mine["sorted_words"][:, j, g, u, :]
-                        else:
+                        if half == FIRST_HALF:
                             columns = slice(g * WORDS_PER_PASS + u, (g + 1) * WORDS_PER_PASS, HALVES)
                             words = x_chunks[c][:, j, :].bitcast(F32)[:, columns]
+                        else:
+                            words = mine["sorted_words"][:, j - SECOND_HALF[0], g, u, :]
                         nc.tensor.transpose(xt[:, g, u, :], words, ident_f32[:])
-                if j in CFG["vector_copies"]:
-                    nc.vector.tensor_copy(
-                        out=mine["grouped"][:, j, :, :, :].bitcast(F32), in_=xt[:].rearrange("p g u k -> p g k u")
-                    )
-                else:
-                    nc.scalar.copy(
-                        out=mine["grouped"][:, j, :, :, :].bitcast(F32), in_=xt[:].rearrange("p g u k -> p g k u")
-                    )
+                nc.scalar.copy(
+                    out=mine["grouped"][:, j, :, :, :].bitcast(F32),
+                    in_=xt[:].rearrange("p g u k -> p g k u"),
+                )
 
         def quantise(c, tiles):
             if not exists(c):
                 return
-            mine = mine_of(c)
-            if "codes" not in mine:
+            mine = buffers_of[c]
+            if tiles == FIRST_HALF:
                 codes = stage.tile([P, TILES, PASSES, P], U32, align_bytes=64)
                 planes = stage.tile([P, TILES, PASSES, P], U8, align_bytes=64)
                 mine["codes"] = codes
                 mine["planes"] = planes
-            both = slice(tiles[0], tiles[-1] + 1)
             nc.vector.quantize_mx(
-                out=mine["codes"][:, both, :, :].rearrange("p j g k -> p (j g k)").bitcast(FP8X4),
-                scales=mine["planes"][:, both, :, :].rearrange("p j g k -> p (j g k)"),
-                in_=mine["grouped"][:, both, :, :, :].rearrange("p j g k t -> p (j g k t)"),
+                out=mine["codes"][:, span(tiles), :, :].rearrange("p j g k -> p (j g k)").bitcast(FP8X4),
+                scales=mine["planes"][:, span(tiles), :, :].rearrange("p j g k -> p (j g k)"),
+                in_=mine["grouped"][:, span(tiles), :, :, :].rearrange("p j g k t -> p (j g k t)"),
             )
 
         def transpose_t(c):
@@ -213,32 +179,26 @@ def tile_linear_pa_t_kernel(tc, data, W_words, W_scales, t_lora, lora_b, out):
             for j in range(TILES):
                 nc.tensor.transpose(tT_ps[:, j, :], t_chunks[c][:, j, :], ident_bf16[:])
             tT = stage.tile([P, TILES, P], BF16)
-            if CFG["t_copy"] == "vector":
-                nc.vector.tensor_copy(out=tT[:], in_=tT_ps[:])
-            else:
-                nc.scalar.copy(out=tT[:], in_=tT_ps[:])
-            mine_of(c)["tT"] = tT
+            nc.vector.tensor_copy(out=tT[:], in_=tT_ps[:])
+            buffers_of[c]["tT"] = tT
 
         def transpose_adapters():
-            lbT_ps = xt_banks.tile([P, ADAPTERS, OUT], BF16, tag="xt")
-            for a in range(ADAPTERS):
-                nc.tensor.transpose(lbT_ps[:, a, :], lb_sb[:, a, :], ident_bf16[:])
-            if CFG["lb_rows"] == "o":
-                nc.scalar.copy(out=lbT[:], in_=lbT_ps[:])
-            else:
-                nc.scalar.copy(
-                    out=lbT[:].rearrange("r a (h i) -> r a h i", i=ADAPTERS),
-                    in_=lbT_ps[:].rearrange("r i (a h) -> r a h i", a=ADAPTERS),
-                )
+            lbT_ps = word_banks.tile([P, ROWS_PER_PARTITION, P], BF16, tag="words")
+            for i in range(ROWS_PER_PARTITION):
+                nc.tensor.transpose(lbT_ps[:, i, :], lb_sb[:, i, :], ident_bf16[:])
+            nc.scalar.copy(
+                out=lbT[:].rearrange("r a (h i) -> r a h i", i=ROWS_PER_PARTITION),
+                in_=lbT_ps[:].rearrange("r i (a h) -> r a h i", a=ADAPTERS),
+            )
 
-        def adapter_product(c, tiles):
+        def adapter_product(c, half):
             if not exists(c):
                 return
-            mine = mine_of(c)
-            if "delta_ps" not in mine:
-                delta_ps = banks.tile([P, TILES, OUT], F32, bufs=CFG["delta_bufs"])
+            mine = buffers_of[c]
+            if half == FIRST_HALF:
+                delta_ps = banks.tile([P, TILES, OUT], F32, bufs=2)
                 mine["delta_ps"] = delta_ps
-            for j in tiles:
+            for j in half:
                 nc.tensor.matmul(
                     mine["delta_ps"][:, j, :],
                     lhsT=mine["tT"][:, j, :],
@@ -250,21 +210,15 @@ def tile_linear_pa_t_kernel(tc, data, W_words, W_scales, t_lora, lora_b, out):
         def base_product_and_store(c):
             if not exists(c):
                 return
-            mine = mine_of(c)
+            mine = buffers_of[c]
             out_sb = resident.tile([P, TILES, OUT], F32)
             nc.scalar.copy(out=out_sb[:], in_=mine["delta_ps"][:])
-            if c == CHUNKS - 1 and CFG["tail"] == "halves":
-                groups = (FIRST_HALF, SECOND_HALF)
-            elif c == CHUNKS - 1 and CFG["tail"] == "fine":
-                groups = (FIRST_HALF, SECOND_HALF[:1], SECOND_HALF[1:])
-            else:
-                groups = (FIRST_HALF + SECOND_HALF,)
-            for n, group in enumerate(groups):
-                if len(groups) == 1:
-                    base_ps = banks.tile([P, TILES, OUT], F32)
+            for tiles in product_groups(c):
+                if c == LAST:
+                    base_ps = word_banks.tile([P, TILES, OUT], F32, tag="words")
                 else:
-                    base_ps = xt_banks.tile([P, TILES, OUT], F32, tag="xt")
-                for j in group:
+                    base_ps = banks.tile([P, TILES, OUT], F32)
+                for j in tiles:
                     for g in range(PASSES):
                         nc.tensor.matmul_mx(
                             out=base_ps[:, j, :],
@@ -275,39 +229,29 @@ def tile_linear_pa_t_kernel(tc, data, W_words, W_scales, t_lora, lora_b, out):
                             start=(g == 0),
                             stop=(g == PASSES - 1),
                         )
-                these = slice(group[0], group[-1] + 1)
                 nc.vector.scalar_tensor_tensor(
-                    out=out_sb[:, these, :], in0=out_sb[:, these, :], scalar=SCALING, in1=base_ps[:, these, :], op0=MULT, op1=ADD
+                    out=out_sb[:, span(tiles), :],
+                    in0=out_sb[:, span(tiles), :],
+                    scalar=SCALING,
+                    in1=base_ps[:, span(tiles), :],
+                    op0=MULT,
+                    op1=ADD,
                 )
-                nc.sync.dma_start(out=chunk_view(out_rows, c)[:, these, :], in_=out_sb[:, these, :])
+                nc.sync.dma_start(out=chunk_view(out_rows, c)[:, span(tiles), :], in_=out_sb[:, span(tiles), :])
 
         def one_round(c):
-            place = CFG["sort_place"]
-            sort_words(c + 1, "gpsimd")
-            if place == "first":
-                sort_words(c + 1, "vector")
-            if CFG["pe_order"] == "after_mx":
-                adapter_product(c - 1, FIRST_HALF)
+            sort_words(c + 1)
             transpose_words(c, FIRST_HALF)
             quantise(c, FIRST_HALF)
-            if place == "mid":
-                sort_words(c + 1, "vector")
-            if CFG["pe_order"] == "middle":
-                adapter_product(c - 1, FIRST_HALF)
+            adapter_product(c - 1, FIRST_HALF)
             transpose_words(c, SECOND_HALF)
             transpose_t(c)
-            if c == CHUNKS - 1 and CFG["tail"] == "fine":
-                quantise(c, SECOND_HALF[:1])
-                quantise(c, SECOND_HALF[1:])
-            else:
-                quantise(c, SECOND_HALF)
-            if place == "late":
-                sort_words(c + 1, "vector")
+            for tiles in quantise_groups(c)[1:]:
+                quantise(c, tiles)
             adapter_product(c - 1, SECOND_HALF)
             base_product_and_store(c - 1)
 
-        sort_words(0, "gpsimd")
-        sort_words(0, "vector")
+        sort_words(0)
         one_round(0)
         transpose_adapters()
         for c in range(1, CHUNKS + 1):

@@ -26,16 +26,21 @@ CHUNK = TILES * P
 CHUNKS = TOKENS // CHUNK
 LAST = CHUNKS - 1
 CHUNKS_PER_ADAPTER = SEQ // CHUNK
-FIRST_HALF = (0, 1)
-SECOND_HALF = (2, 3)
+STEPPED_TILES = (0, 1)
+SORTED_TILES = (2, 3)
 QUADRANTS = 4
 ROWS_PER_PARTITION = ADAPTERS * OUT // P
 
 FLOPS = 2 * TOKENS * IN * OUT + 2 * TOKENS * RANK * OUT
 
 
+def adapter_view(rows, a):
+    return rows[a * SEQ : (a + 1) * SEQ, :].rearrange("(p n) w -> p n w", n=CHUNKS_PER_ADAPTER * TILES)
+
+
 def chunk_view(rows, c):
-    return rows[c * CHUNK : (c + 1) * CHUNK, :].rearrange("(p j) w -> p j w", j=TILES)
+    first = (c % CHUNKS_PER_ADAPTER) * TILES
+    return adapter_view(rows, c // CHUNKS_PER_ADAPTER)[:, first : first + TILES, :]
 
 
 def span(tiles):
@@ -44,14 +49,14 @@ def span(tiles):
 
 def quantise_groups(c):
     if c == LAST:
-        return (FIRST_HALF, SECOND_HALF[:1], SECOND_HALF[1:])
-    return (FIRST_HALF, SECOND_HALF)
+        return (STEPPED_TILES, SORTED_TILES[:1], SORTED_TILES[1:])
+    return (STEPPED_TILES, SORTED_TILES)
 
 
 def product_groups(c):
     if c == LAST:
         return quantise_groups(c)
-    return (FIRST_HALF + SECOND_HALF,)
+    return (STEPPED_TILES + SORTED_TILES,)
 
 
 def tile_linear_pa_t_kernel(tc, data, W_words, W_scales, t_lora, lora_b, out):
@@ -87,9 +92,11 @@ def tile_linear_pa_t_kernel(tc, data, W_words, W_scales, t_lora, lora_b, out):
             x_chunks.append(x_sb)
 
         def load_t(c):
-            t_sb = resident.tile([P, TILES, RANK], BF16)
-            nc.sync.dma_start(out=t_sb[:], in_=chunk_view(t_rows, c))
-            t_chunks.append(t_sb)
+            if c % CHUNKS_PER_ADAPTER == 0:
+                t_sb = resident.tile([P, CHUNKS_PER_ADAPTER * TILES, RANK], BF16)
+                nc.sync.dma_start(out=t_sb[:], in_=adapter_view(t_rows, c // CHUNKS_PER_ADAPTER))
+                for h in range(CHUNKS_PER_ADAPTER):
+                    t_chunks.append(t_sb[:, h * TILES : (h + 1) * TILES, :])
 
         def load_adapters():
             nc.sync.dma_start(
@@ -126,31 +133,31 @@ def tile_linear_pa_t_kernel(tc, data, W_words, W_scales, t_lora, lora_b, out):
         def sort_words(c):
             if not exists(c):
                 return
-            sorted_words = stage.tile([P, len(SECOND_HALF), PASSES, HALVES, P], F32)
+            sorted_words = stage.tile([P, len(SORTED_TILES), PASSES, HALVES, P], F32)
             nc.vector.tensor_copy(
                 out=sorted_words[:],
-                in_=x_chunks[c][:, span(SECOND_HALF), :]
+                in_=x_chunks[c][:, span(SORTED_TILES), :]
                 .bitcast(F32)
                 .rearrange("p j (g q u) -> p j g u q", g=PASSES, u=HALVES),
             )
             buffers_of[c] = {"sorted_words": sorted_words}
 
-        def transpose_words(c, half):
+        def transpose_words(c, tiles):
             if not exists(c):
                 return
             mine = buffers_of[c]
-            if half == FIRST_HALF:
+            if tiles == STEPPED_TILES:
                 grouped = stage.tile([P, TILES, PASSES, P, PACK], BF16, align_bytes=64)
                 mine["grouped"] = grouped
-            for j in half:
+            for j in tiles:
                 xt = word_banks.tile([P, PASSES, HALVES, P], F32, tag="words")
                 for g in range(PASSES):
                     for u in range(HALVES):
-                        if half == FIRST_HALF:
+                        if tiles == STEPPED_TILES:
                             columns = slice(g * WORDS_PER_PASS + u, (g + 1) * WORDS_PER_PASS, HALVES)
                             words = x_chunks[c][:, j, :].bitcast(F32)[:, columns]
                         else:
-                            words = mine["sorted_words"][:, j - SECOND_HALF[0], g, u, :]
+                            words = mine["sorted_words"][:, j - SORTED_TILES[0], g, u, :]
                         nc.tensor.transpose(xt[:, g, u, :], words, ident_f32[:])
                 nc.scalar.copy(
                     out=mine["grouped"][:, j, :, :, :].bitcast(F32),
@@ -161,7 +168,7 @@ def tile_linear_pa_t_kernel(tc, data, W_words, W_scales, t_lora, lora_b, out):
             if not exists(c):
                 return
             mine = buffers_of[c]
-            if tiles == FIRST_HALF:
+            if tiles == STEPPED_TILES:
                 codes = stage.tile([P, TILES, PASSES, P], U32, align_bytes=64)
                 planes = stage.tile([P, TILES, PASSES, P], U8, align_bytes=64)
                 mine["codes"] = codes
@@ -191,14 +198,14 @@ def tile_linear_pa_t_kernel(tc, data, W_words, W_scales, t_lora, lora_b, out):
                 in_=lbT_ps[:].rearrange("r i (a h) -> r a h i", a=ADAPTERS),
             )
 
-        def adapter_product(c, half):
+        def adapter_product(c, tiles):
             if not exists(c):
                 return
             mine = buffers_of[c]
-            if half == FIRST_HALF:
+            if tiles == STEPPED_TILES:
                 delta_ps = banks.tile([P, TILES, OUT], F32, bufs=2)
                 mine["delta_ps"] = delta_ps
-            for j in half:
+            for j in tiles:
                 nc.tensor.matmul(
                     mine["delta_ps"][:, j, :],
                     lhsT=mine["tT"][:, j, :],
@@ -241,14 +248,14 @@ def tile_linear_pa_t_kernel(tc, data, W_words, W_scales, t_lora, lora_b, out):
 
         def one_round(c):
             sort_words(c + 1)
-            transpose_words(c, FIRST_HALF)
-            quantise(c, FIRST_HALF)
-            adapter_product(c - 1, FIRST_HALF)
-            transpose_words(c, SECOND_HALF)
+            transpose_words(c, STEPPED_TILES)
+            quantise(c, STEPPED_TILES)
+            adapter_product(c - 1, STEPPED_TILES)
+            transpose_words(c, SORTED_TILES)
             transpose_t(c)
             for tiles in quantise_groups(c)[1:]:
                 quantise(c, tiles)
-            adapter_product(c - 1, SECOND_HALF)
+            adapter_product(c - 1, SORTED_TILES)
             base_product_and_store(c - 1)
 
         sort_words(0)

from contextlib import ExitStack

import concourse.mybir as mybir
from concourse.masks import make_identity

BF16 = mybir.dt.bfloat16
F32 = mybir.dt.float32
I32 = mybir.dt.int32
U8 = mybir.dt.uint8
U32 = mybir.dt.uint32
FP8X4 = mybir.dt.float8_e4m3fn_x4
FP4X4 = mybir.dt.float4_e2m1fn_x4
MULT = mybir.AluOpType.mult
ADD = mybir.AluOpType.add

P = 128
PACK = 4
HALVES = 2
ADAPTERS, SEQ, IN, OUT, RANK = 8, 1024, 1024, 128, 128
SCALING = 2.0
TOKENS = ADAPTERS * SEQ
PASSES = IN // (P * PACK)
WORDS_PER_PASS = P * HALVES
TILES = 4
CHUNK = TILES * P
CHUNKS = TOKENS // CHUNK
LAST = CHUNKS - 1
CHUNKS_PER_ADAPTER = SEQ // CHUNK
STEPPED_TILES = (0, 1)
SORTED_TILES = (2, 3)
QUADRANTS = 4
ROWS_PER_PARTITION = ADAPTERS * OUT // P

FLOPS = 2 * TOKENS * IN * OUT + 2 * TOKENS * RANK * OUT


def adapter_view(rows, a):
    return rows[a * SEQ : (a + 1) * SEQ, :].rearrange("(p n) w -> p n w", n=CHUNKS_PER_ADAPTER * TILES)


def chunk_view(rows, c):
    first = (c % CHUNKS_PER_ADAPTER) * TILES
    return adapter_view(rows, c // CHUNKS_PER_ADAPTER)[:, first : first + TILES, :]


def span(tiles):
    return slice(tiles[0], tiles[-1] + 1)


def quantise_groups(c):
    if c == LAST:
        return (STEPPED_TILES, SORTED_TILES[:1], SORTED_TILES[1:])
    return (STEPPED_TILES, SORTED_TILES)


def product_groups(c):
    if c == LAST:
        return quantise_groups(c)
    return (STEPPED_TILES + SORTED_TILES,)


def tile_linear_pa_t_kernel(tc, data, W_words, W_scales, t_lora, lora_b, out):
    nc = tc.nc
    x_rows = data.rearrange("b s i -> (b s) i")
    t_rows = t_lora.rearrange("a g s r -> (a g s) r")
    out_rows = out.rearrange("b s o -> (b s) o")

    with ExitStack() as ctx:
        ctx.enter_context(tc.manual_schedule())
        const = ctx.enter_context(tc.tile_pool(name="const", bufs=1))
        resident = ctx.enter_context(tc.tile_pool(name="resident", bufs=CHUNKS))
        stage = ctx.enter_context(tc.tile_pool(name="stage", bufs=2))
        word_banks = ctx.enter_context(tc.psum_pool(name="word_banks", bufs=TILES))
        banks = ctx.enter_context(tc.psum_pool(name="banks", bufs=1))

        w_planes = const.tile([P, PASSES, OUT], U8, align_bytes=64)
        nc.vector.memset(w_planes[:].bitcast(I32), 0)
        w_words = const.tile([P, PASSES, 2 * OUT], U8, align_bytes=64)
        lb_sb = const.tile([P, ROWS_PER_PARTITION, RANK], BF16)
        lbT = const.tile([P, ADAPTERS, OUT], BF16)
        ident_f32 = const.tile([P, P], F32)
        make_identity(nc, ident_f32[:])
        ident_bf16 = const.tile([P, P], BF16)
        make_identity(nc, ident_bf16[:])

        x_chunks = []
        t_chunks = []

        def load_x(c):
            x_sb = resident.tile([P, TILES, IN], BF16)
            nc.sync.dma_start(out=x_sb[:], in_=chunk_view(x_rows, c))
            x_chunks.append(x_sb)

        def load_t(c):
            if c % CHUNKS_PER_ADAPTER == 0:
                t_sb = resident.tile([P, CHUNKS_PER_ADAPTER * TILES, RANK], BF16)
                nc.sync.dma_start(out=t_sb[:], in_=adapter_view(t_rows, c // CHUNKS_PER_ADAPTER))
                for h in range(CHUNKS_PER_ADAPTER):
                    t_chunks.append(t_sb[:, h * TILES : (h + 1) * TILES, :])

        def load_adapters():
            nc.sync.dma_start(
                out=lb_sb[:], in_=lora_b.rearrange("a (h i) r -> (a h) i r", i=ROWS_PER_PARTITION)
            )

        def load_weights():
            nc.sync.dma_start(
                out=w_words[:].bitcast(I32), in_=W_words.rearrange("g p b -> p g b").bitcast(I32)
            )
            for quadrant in range(QUADRANTS):
                nc.sync.dma_start(
                    out=w_planes[32 * quadrant : 32 * quadrant + 4, :, :].bitcast(I32),
                    in_=W_scales[:, 4 * quadrant : 4 * quadrant + 4, :]
                    .rearrange("g r o -> r g o")
                    .bitcast(I32),
                )

        load_x(0)
        load_t(0)
        load_adapters()
        load_x(1)
        load_weights()
        load_t(1)
        for c in range(2, CHUNKS):
            load_x(c)
            load_t(c)

        buffers_of = {}

        def exists(c):
            return 0 <= c < CHUNKS

        def sort_words(c):
            if not exists(c):
                return
            sorted_words = stage.tile([P, len(SORTED_TILES), PASSES, HALVES, P], F32)
            nc.vector.tensor_copy(
                out=sorted_words[:],
                in_=x_chunks[c][:, span(SORTED_TILES), :]
                .bitcast(F32)
                .rearrange("p j (g q u) -> p j g u q", g=PASSES, u=HALVES),
            )
            buffers_of[c] = {"sorted_words": sorted_words}

        def transpose_words(c, tiles):
            if not exists(c):
                return
            mine = buffers_of[c]
            if tiles == STEPPED_TILES:
                grouped = stage.tile([P, TILES, PASSES, P, PACK], BF16, align_bytes=64)
                mine["grouped"] = grouped
            for j in tiles:
                xt = word_banks.tile([P, PASSES, HALVES, P], F32, tag="words")
                for g in range(PASSES):
                    for u in range(HALVES):
                        if tiles == STEPPED_TILES:
                            columns = slice(g * WORDS_PER_PASS + u, (g + 1) * WORDS_PER_PASS, HALVES)
                            words = x_chunks[c][:, j, :].bitcast(F32)[:, columns]
                        else:
                            words = mine["sorted_words"][:, j - SORTED_TILES[0], g, u, :]
                        nc.tensor.transpose(xt[:, g, u, :], words, ident_f32[:])
                nc.scalar.copy(
                    out=mine["grouped"][:, j, :, :, :].bitcast(F32),
                    in_=xt[:].rearrange("p g u k -> p g k u"),
                )

        def quantise(c, tiles):
            if not exists(c):
                return
            mine = buffers_of[c]
            if tiles == STEPPED_TILES:
                codes = stage.tile([P, TILES, PASSES, P], U32, align_bytes=64)
                planes = stage.tile([P, TILES, PASSES, P], U8, align_bytes=64)
                mine["codes"] = codes
                mine["planes"] = planes
            nc.vector.quantize_mx(
                out=mine["codes"][:, span(tiles), :, :].rearrange("p j g k -> p (j g k)").bitcast(FP8X4),
                scales=mine["planes"][:, span(tiles), :, :].rearrange("p j g k -> p (j g k)"),
                in_=mine["grouped"][:, span(tiles), :, :, :].rearrange("p j g k t -> p (j g k t)"),
            )

        def transpose_t(c):
            if not exists(c):
                return
            tT_ps = banks.tile([P, TILES, P], BF16)
            for j in range(TILES):
                nc.tensor.transpose(tT_ps[:, j, :], t_chunks[c][:, j, :], ident_bf16[:])
            tT = stage.tile([P, TILES, P], BF16)
            nc.vector.tensor_copy(out=tT[:], in_=tT_ps[:])
            buffers_of[c]["tT"] = tT

        def transpose_adapters():
            lbT_ps = word_banks.tile([P, ROWS_PER_PARTITION, P], BF16, tag="words")
            for i in range(ROWS_PER_PARTITION):
                nc.tensor.transpose(lbT_ps[:, i, :], lb_sb[:, i, :], ident_bf16[:])
            nc.scalar.copy(
                out=lbT[:].rearrange("r a (h i) -> r a h i", i=ROWS_PER_PARTITION),
                in_=lbT_ps[:].rearrange("r i (a h) -> r a h i", a=ADAPTERS),
            )

        def adapter_product(c, tiles):
            if not exists(c):
                return
            mine = buffers_of[c]
            if tiles == STEPPED_TILES:
                delta_ps = banks.tile([P, TILES, OUT], F32, bufs=2)
                mine["delta_ps"] = delta_ps
            for j in tiles:
                nc.tensor.matmul(
                    mine["delta_ps"][:, j, :],
                    lhsT=mine["tT"][:, j, :],
                    rhs=lbT[:, c // CHUNKS_PER_ADAPTER, :],
                    start=True,
                    stop=True,
                )

        def base_product_and_store(c):
            if not exists(c):
                return
            mine = buffers_of[c]
            out_sb = resident.tile([P, TILES, OUT], F32)
            nc.scalar.copy(out=out_sb[:], in_=mine["delta_ps"][:])
            for tiles in product_groups(c):
                if c == LAST:
                    base_ps = word_banks.tile([P, TILES, OUT], F32, tag="words")
                else:
                    base_ps = banks.tile([P, TILES, OUT], F32)
                for j in tiles:
                    for g in range(PASSES):
                        nc.tensor.matmul_mx(
                            out=base_ps[:, j, :],
                            lhsT=mine["codes"][:, j, g, :].bitcast(FP8X4),
                            lhsT_scale=mine["planes"][:, j, g, :],
                            rhs=w_words[:, g, :].bitcast(FP4X4),
                            rhs_scale=w_planes[:, g, :],
                            start=(g == 0),
                            stop=(g == PASSES - 1),
                        )
                nc.vector.scalar_tensor_tensor(
                    out=out_sb[:, span(tiles), :],
                    in0=out_sb[:, span(tiles), :],
                    scalar=SCALING,
                    in1=base_ps[:, span(tiles), :],
                    op0=MULT,
                    op1=ADD,
                )
                nc.sync.dma_start(out=chunk_view(out_rows, c)[:, span(tiles), :], in_=out_sb[:, span(tiles), :])

        def one_round(c):
            sort_words(c + 1)
            transpose_words(c, STEPPED_TILES)
            quantise(c, STEPPED_TILES)
            adapter_product(c - 1, STEPPED_TILES)
            transpose_words(c, SORTED_TILES)
            transpose_t(c)
            for tiles in quantise_groups(c)[1:]:
                quantise(c, tiles)
            adapter_product(c - 1, SORTED_TILES)
            base_product_and_store(c - 1)

        sort_words(0)
        one_round(0)
        transpose_adapters()
        for c in range(1, CHUNKS + 1):
            one_round(c)
